import numpy as np
import ml_dtypes


def mxq(x, axis, fmt="e4m3"):
    dtype, down = {"e4m3": (ml_dtypes.float8_e4m3fn, 7), "e5m2": (ml_dtypes.float8_e5m2, 14)}[fmt]
    v = np.moveaxis(np.asarray(x, np.float32).astype(ml_dtypes.bfloat16).astype(np.float64), axis, -1)
    blocks = v.reshape(v.shape[:-1] + (-1, 32))
    amax = np.abs(blocks).max(-1, keepdims=True)
    byte = np.maximum(np.where(amax > 0, np.frexp(amax)[1] - 1 + 127, 0) - down, 1)
    scale = np.exp2(byte - 127.0)
    codes = (blocks / scale).astype(np.float32).astype(dtype).astype(np.float64)
    return np.moveaxis((codes * scale).reshape(v.shape), -1, axis)


WIDE = False


def mx_kscale(k):
    if not WIDE:
        return np.ones(k)
    levels = np.array([10, -10, 5, -5, 0])
    a = np.random.permutation(np.resize(levels, k // 512 * 4)).reshape(k // 512, 4)
    idx = np.arange(k)
    return np.exp2(a[idx // 512, idx % 128 // 32])


BF16 = ml_dtypes.bfloat16


def bf(x):
    return np.asarray(x, np.float32).astype(BF16)


def f64(x):
    return np.asarray(x).astype(np.float64)


E2M1 = np.array([0.0, 0.5, 1.0, 1.5, 2.0, 3.0, 4.0, 6.0, -0.0, -0.5, -1.0, -1.5, -2.0, -3.0, -4.0, -6.0])


def pack_weight(w, fmt):
    k, n = w.shape
    w = f64(bf(w)).reshape(k // 32, 32, n)
    amax = np.abs(w).max(1)
    if fmt == "e4m3":
        byte = np.frexp(amax)[1] - 1 + 127 - 7
    else:
        mant, ex = np.frexp(amax / 6.0)
        byte = np.where(mant > 0.5, ex, ex - 1) + 127
    byte = np.clip(np.where(amax > 0, byte, 1), 1, 254)
    scaled = (w * np.exp2(127.0 - byte)[:, None, :]).reshape(k, n).astype(np.float32)
    by_word = np.ascontiguousarray(scaled.reshape(k // 512, 128, 4, n).transpose(0, 1, 3, 2))
    if fmt == "e4m3":
        words = by_word.astype(ml_dtypes.float8_e4m3fn).view(np.uint8)
    else:
        c = by_word.astype(ml_dtypes.float4_e2m1fn).view(np.uint8) & 0xF
        words = c[..., 0::2] | (c[..., 1::2] << 4)
    return np.ascontiguousarray(words), np.ascontiguousarray(byte.astype(np.uint8).reshape(k // 512, 16, n))


def unpack_weight(words, scales, fmt):
    g, p, n, _ = words.shape
    if fmt == "e4m3":
        vals = np.ascontiguousarray(words).view(ml_dtypes.float8_e4m3fn).astype(np.float64)
    else:
        nib = np.empty((g, p, n, 4), np.uint8)
        nib[..., 0::2] = words & 0xF
        nib[..., 1::2] = words >> 4
        vals = E2M1[nib]
    vals = vals * np.repeat(np.exp2(scales.astype(np.float64) - 127.0), 8, axis=1)[..., None]
    return vals.transpose(0, 1, 3, 2).reshape(g * 512, n)


M, SP, H, FF, NH = 512, 384, 1024, 2560, 8
EPS = 1.1920929e-07
G = 2


def rms_norm(x, w):
    var = np.mean(np.square(x), axis=-1, keepdims=True)
    return x * (1.0 / np.sqrt(var + EPS)) * w


def silu(v):
    return v / (1.0 + np.exp(-v))


def setup_inputs():
    s, t = mx_kscale(H), mx_kscale(H)
    attn = bf(np.random.standard_normal((M, H)) * 0.25 * s)
    x = bf(np.random.standard_normal((M, H)))
    W_o = np.random.standard_normal((G, H, H)) * 2.0 / np.sqrt(H) / s[None, :, None]
    W_gu = np.random.standard_normal((G, H, 2 * FF)) / np.sqrt(H) / t[None, :, None]
    ln2 = bf((1.0 + 0.1 * np.random.standard_normal((G, H))) * t)
    W_o_words, W_o_scales = pack_weight(W_o.reshape(-1, H), "e4m3")
    W_gu_words, W_gu_scales = pack_weight(W_gu.reshape(-1, 2 * FF), "e4m3")
    return {"attn": attn,
            "x": x,
            "W_o_words": W_o_words,
            "W_o_scales": W_o_scales,
            "W_gu_words": W_gu_words,
            "W_gu_scales": W_gu_scales,
            "ln2": ln2}


def reference(attn, x, W_o_words, W_o_scales, W_gu_words, W_gu_scales, ln2):
    attn, x, ln2 = f64(attn), f64(x), f64(ln2)
    W_o = unpack_weight(W_o_words, W_o_scales, "e4m3").reshape(G, H, H)
    W_gu = unpack_weight(W_gu_words, W_gu_scales, "e4m3").reshape(G, H, 2 * FF)
    o0 = mxq(attn[:SP], 1, "e4m3") @ W_o[0]
    o1 = mxq(attn[SP:], 1, "e4m3") @ W_o[1]
    x_mid = x + np.concatenate([o0, o1], axis=0)
    h0 = rms_norm(x_mid[:SP], ln2[0])
    h1 = rms_norm(x_mid[SP:], ln2[1])
    gu0 = mxq(h0, 1, "e4m3") @ W_gu[0]
    gu1 = mxq(h1, 1, "e4m3") @ W_gu[1]
    gu = np.concatenate([gu0, gu1], axis=0)
    gate, up = np.split(gu, 2, axis=-1)
    return x_mid, silu(gate) * up

@@ -1,0 +1,240 @@
+from contextlib import ExitStack
+
+import concourse.mybir as mybir
+from concourse.masks import make_identity
+
+F32 = mybir.dt.float32
+BF16 = mybir.dt.bfloat16
+I32 = mybir.dt.int32
+U32 = mybir.dt.uint32
+U8 = mybir.dt.uint8
+FP8X4 = mybir.dt.float8_e4m3fn_x4
+ACT = mybir.ActivationFunctionType
+ALU = mybir.AluOpType
+
+P = 128
+ROWS, SPLIT, H, FF = 512, 384, 1024, 2560
+MODELS = 2
+EPS = 1.1920929e-07
+PACK = 4
+K_PASS = P * PACK
+PASSES = H // K_PASS
+N_BLOCK = 512
+ROW_TILES = ROWS // P
+MODEL_OF_ROW_TILE = tuple(0 if P * rt < SPLIT else 1 for rt in range(ROW_TILES))
+ROW_TILES_OF_MODEL = tuple(
+    tuple(rt for rt in range(ROW_TILES) if MODEL_OF_ROW_TILE[rt] == model) for model in range(MODELS)
+)
+FF_BLOCKS = FF // N_BLOCK
+GU_CHUNKS = (((0, 2), (2, FF_BLOCKS)), ((0, FF_BLOCKS),))
+
+FLOPS = 2 * ROWS * H * H + 2 * ROWS * H * 2 * FF
+
+
+def tile_twomodelblockrouted_pb_e_kernel(
+    tc, attn, x, W_o_words, W_o_scales, W_gu_words, W_gu_scales, ln2, out_0, out_1
+):
+    nc = tc.nc
+    with ExitStack() as stack:
+        stack.enter_context(tc.manual_schedule())
+        keep = stack.enter_context(tc.tile_pool(name="keep", bufs=1))
+        work = stack.enter_context(tc.tile_pool(name="work", bufs=3))
+        banks = stack.enter_context(tc.psum_pool(name="banks", bufs=8))
+
+        wo_planes = keep.tile([P, H], U8, align_bytes=64)
+        wgu_planes = keep.tile([P, 2 * FF], U8, align_bytes=64)
+        ln2_row = keep.tile([P, MODELS * H], BF16)
+        ones = keep.tile([P, P], BF16)
+        eps = keep.tile([P, 1], F32)
+        ident = keep.tile([P, P], F32)
+        nc.vector.memset(wo_planes[:].bitcast(I32), 0)
+        nc.vector.memset(ln2_row[:], 0.0)
+        nc.vector.memset(ones[:], 1.0)
+        nc.vector.memset(eps[:], EPS)
+        nc.vector.memset(wgu_planes[:].bitcast(I32), 0)
+        make_identity(nc, ident[:])
+
+        def load_planes(planes, scales):
+            for quadrant in range(4):
+                nc.sync.dma_start(
+                    out=planes[32 * quadrant : 32 * quadrant + 16, :].bitcast(I32),
+                    in_=scales[:, 4 * quadrant : 4 * quadrant + 4, :].bitcast(I32),
+                )
+
+        def load_wo(group):
+            nc.sync.dma_start(
+                out=wo_words[group][:].bitcast(I32),
+                in_=W_o_words[group].rearrange("p n t -> p (n t)").bitcast(I32),
+            )
+
+        attn_sb = [keep.tile([P, H], BF16, name="attn_%d" % rt) for rt in range(ROW_TILES)]
+        x_sb = [keep.tile([P, H], BF16, name="x_%d" % rt) for rt in range(ROW_TILES)]
+        wo_words = [
+            keep.tile([P, H], U32, name="wo_%d" % group, align_bytes=64)
+            for group in range(MODELS * PASSES)
+        ]
+        wgu_words = {}
+
+        nc.scalar.dma_start(out=ln2_row[0:1, :], in_=ln2.rearrange("e k -> (e k)").unsqueeze(0))
+        for rt in range(ROW_TILES):
+            nc.sync.dma_start(out=attn_sb[rt][:], in_=attn[P * rt : P * (rt + 1), :])
+        load_planes(wo_planes, W_o_scales)
+        for g in range(PASSES):
+            load_wo(g)
+        for rt in range(ROW_TILES):
+            nc.sync.dma_start(out=x_sb[rt][:], in_=x[P * rt : P * (rt + 1), :])
+        for g in range(PASSES):
+            load_wo(PASSES + g)
+        load_planes(wgu_planes, W_gu_scales)
+        for model in range(MODELS):
+            for first, last in GU_CHUNKS[model]:
+                for g in range(PASSES):
+                    group = PASSES * model + g
+                    chunk = keep.tile(
+                        [P, 2, (last - first) * N_BLOCK],
+                        U32,
+                        name="wgu_%d_%d" % (group, first),
+                        align_bytes=64,
+                    )
+                    wgu_words[(group, first)] = chunk
+                    halves = W_gu_words[group].rearrange("p (s n) t -> p s (n t)", s=2)
+                    nc.sync.dma_start(
+                        out=chunk[:].bitcast(I32),
+                        in_=halves[:, :, PACK * N_BLOCK * first : PACK * N_BLOCK * last].bitcast(I32),
+                    )
+
+        def quantise_rows(rows_bf16, codes, planes):
+            words = rows_bf16[:].bitcast(F32)
+            turned = banks.tile([P, PASSES, 2, P], F32, tag="bank")
+            for g in range(PASSES):
+                for u in range(2):
+                    nc.tensor.transpose(
+                        turned[:, g, u, :], words[:, 256 * g + u : 256 * (g + 1) : 2], ident[:]
+                    )
+            grouped = work.tile([P, PASSES, P, PACK], BF16, align_bytes=64)
+            nc.scalar.copy(
+                out=grouped[:].bitcast(F32), in_=turned[:].rearrange("p g u r -> p g r u")
+            )
+            nc.vector.quantize_mx(
+                out=codes[:].rearrange("p g r -> p (g r)").bitcast(FP8X4),
+                scales=planes[:].rearrange("p g r -> p (g r)"),
+                in_=grouped[:].rearrange("p g r t -> p (g r t)"),
+            )
+
+        def mx_operand(name):
+            codes = [
+                keep.tile([P, PASSES, P], U32, name="%s_codes_%d" % (name, rt), align_bytes=64)
+                for rt in range(ROW_TILES)
+            ]
+            planes = [
+                keep.tile([P, PASSES, P], U8, name="%s_planes_%d" % (name, rt), align_bytes=64)
+                for rt in range(ROW_TILES)
+            ]
+            return codes, planes
+
+        a_codes, a_planes = mx_operand("a")
+        h_codes, h_planes = mx_operand("h")
+
+        for rt in range(ROW_TILES):
+            quantise_rows(attn_sb[rt], a_codes[rt], a_planes[rt])
+
+        gains = keep.tile([P, MODELS, H], BF16)
+        for model in range(MODELS):
+            for nb in range(H // N_BLOCK):
+                spread = banks.tile([P, N_BLOCK], F32, tag="bank")
+                nc.tensor.matmul(
+                    out=spread[:],
+                    lhsT=ones[:],
+                    rhs=ln2_row[:, H * model + N_BLOCK * nb : H * model + N_BLOCK * (nb + 1)],
+                    start=True,
+                    stop=True,
+                )
+                nc.scalar.copy(out=gains[:, model, N_BLOCK * nb : N_BLOCK * (nb + 1)], in_=spread[:])
+
+        xmid = [keep.tile([P, H], F32, name="xmid_%d" % rt) for rt in range(ROW_TILES)]
+        sumsq = keep.tile([P, ROW_TILES], F32)
+        rms = keep.tile([P, ROW_TILES], F32)
+        rstd = keep.tile([P, ROW_TILES], F32)
+        for rt in range(ROW_TILES):
+            for nb in range(H // N_BLOCK):
+                cols = slice(N_BLOCK * nb, N_BLOCK * (nb + 1))
+                o_acc = banks.tile([P, N_BLOCK], F32, tag="bank")
+                for g in range(PASSES):
+                    group = PASSES * MODEL_OF_ROW_TILE[rt] + g
+                    nc.tensor.matmul_mx(
+                        out=o_acc[:],
+                        lhsT=a_codes[rt][:, g, :].bitcast(FP8X4),
+                        lhsT_scale=a_planes[rt][:, g, :],
+                        rhs=wo_words[group][:, cols].bitcast(FP8X4),
+                        rhs_scale=wo_planes[4 * group : P, cols],
+                        start=(g == 0),
+                        stop=(g == PASSES - 1),
+                    )
+                nc.vector.tensor_tensor(
+                    out=xmid[rt][:, cols], in0=o_acc[:], in1=x_sb[rt][:, cols], op=ALU.add
+                )
+            squares = work.tile([P, H], BF16)
+            nc.scalar.activation(
+                out=squares[:], in_=xmid[rt][:], func=ACT.Square, accum_out=sumsq[:, rt : rt + 1]
+            )
+            nc.scalar.activation(
+                out=rms[:, rt : rt + 1],
+                in_=sumsq[:, rt : rt + 1],
+                func=ACT.Sqrt,
+                scale=1.0 / H,
+                bias=eps[:],
+            )
+
+        h_sb = [keep.tile([P, H], BF16, name="h_%d" % rt) for rt in range(ROW_TILES)]
+        for rt in range(ROW_TILES):
+            nc.vector.reciprocal(out=rstd[:, rt : rt + 1], in_=rms[:, rt : rt + 1])
+            nc.vector.scalar_tensor_tensor(
+                out=h_sb[rt][:],
+                in0=xmid[rt][:],
+                scalar=rstd[:, rt : rt + 1],
+                in1=gains[:, MODEL_OF_ROW_TILE[rt], :],
+                op0=ALU.mult,
+                op1=ALU.mult,
+            )
+        for rt in range(ROW_TILES):
+            quantise_rows(h_sb[rt], h_codes[rt], h_planes[rt])
+
+        def project(rt, first, blk, side):
+            acc = banks.tile([P, N_BLOCK], F32, tag="bank")
+            for g in range(PASSES):
+                group = PASSES * MODEL_OF_ROW_TILE[rt] + g
+                nc.tensor.matmul_mx(
+                    out=acc[:],
+                    lhsT=h_codes[rt][:, g, :].bitcast(FP8X4),
+                    lhsT_scale=h_planes[rt][:, g, :],
+                    rhs=wgu_words[(group, first)][
+                        :, side, N_BLOCK * (blk - first) : N_BLOCK * (blk - first + 1)
+                    ].bitcast(FP8X4),
+                    rhs_scale=wgu_planes[
+                        4 * group : P, FF * side + N_BLOCK * blk : FF * side + N_BLOCK * (blk + 1)
+                    ],
+                    start=(g == 0),
+                    stop=(g == PASSES - 1),
+                )
+            return acc
+
+        hmlp = [keep.tile([P, FF], F32, name="hmlp_%d" % rt) for rt in range(ROW_TILES)]
+        for model in range(MODELS):
+            for first, last in GU_CHUNKS[model]:
+                for rt in ROW_TILES_OF_MODEL[model]:
+                    for blk in range(first, last):
+                        gate = project(rt, first, blk, 0)
+                        up = project(rt, first, blk, 1)
+                        silu_gate = work.tile([P, N_BLOCK], F32)
+                        nc.scalar.activation(out=silu_gate[:], in_=gate[:], func=ACT.Silu)
+                        nc.vector.tensor_tensor(
+                            out=hmlp[rt][:, N_BLOCK * blk : N_BLOCK * (blk + 1)],
+                            in0=silu_gate[:],
+                            in1=up[:],
+                            op=ALU.mult,
+                        )
+
+        for rt in range(ROW_TILES):
+            nc.sync.dma_start(out=out_0[P * rt : P * (rt + 1), :], in_=xmid[rt][:])
+        for rt in range(ROW_TILES):
+            nc.sync.dma_start(out=out_1[P * rt : P * (rt + 1), :], in_=hmlp[rt][:])

@@ -20,11 +20,9 @@ PACK = 4
 K_PASS = P * PACK
 PASSES = H // K_PASS
 N_BLOCK = 512
-ROW_TILES = ROWS // P
-MODEL_OF_ROW_TILE = tuple(0 if P * rt < SPLIT else 1 for rt in range(ROW_TILES))
-ROW_TILES_OF_MODEL = tuple(
-    tuple(rt for rt in range(ROW_TILES) if MODEL_OF_ROW_TILE[rt] == model) for model in range(MODELS)
-)
+FIRST_ROW = (0, SPLIT, ROWS)
+TILES_OF_MODEL = tuple((FIRST_ROW[e + 1] - FIRST_ROW[e]) // P for e in range(MODELS))
+ROW_TILES = tuple((e, t) for e in range(MODELS) for t in range(TILES_OF_MODEL[e]))
 FF_BLOCKS = FF // N_BLOCK
 GU_CHUNKS = (((0, 2), (2, FF_BLOCKS)), ((0, FF_BLOCKS),))
 
@@ -67,8 +65,19 @@ def tile_twomodelblockrouted_pb_e_kernel(
                 in_=W_o_words[group].rearrange("p n t -> p (n t)").bitcast(I32),
             )
 
-        attn_sb = [keep.tile([P, H], BF16, name="attn_%d" % rt) for rt in range(ROW_TILES)]
-        x_sb = [keep.tile([P, H], BF16, name="x_%d" % rt) for rt in range(ROW_TILES)]
+        def rows_of(dram, model):
+            return dram[FIRST_ROW[model] : FIRST_ROW[model + 1], :].rearrange(
+                "(p t) c -> p t c", t=TILES_OF_MODEL[model]
+            )
+
+        def per_model(name, width, dtype):
+            return [
+                keep.tile([P, TILES_OF_MODEL[e], width], dtype, name="%s_%d" % (name, e))
+                for e in range(MODELS)
+            ]
+
+        attn_sb = per_model("attn", H, BF16)
+        x_sb = per_model("x", H, BF16)
         wo_words = [
             keep.tile([P, H], U32, name="wo_%d" % group, align_bytes=64)
             for group in range(MODELS * PASSES)
@@ -76,13 +85,13 @@ def tile_twomodelblockrouted_pb_e_kernel(
         wgu_words = {}
 
         nc.scalar.dma_start(out=ln2_row[0:1, :], in_=ln2.rearrange("e k -> (e k)").unsqueeze(0))
-        for rt in range(ROW_TILES):
-            nc.sync.dma_start(out=attn_sb[rt][:], in_=attn[P * rt : P * (rt + 1), :])
+        for model in range(MODELS):
+            nc.sync.dma_start(out=attn_sb[model][:], in_=rows_of(attn, model))
         load_planes(wo_planes, W_o_scales)
         for g in range(PASSES):
             load_wo(g)
-        for rt in range(ROW_TILES):
-            nc.sync.dma_start(out=x_sb[rt][:], in_=x[P * rt : P * (rt + 1), :])
+        for model in range(MODELS):
+            nc.sync.dma_start(out=x_sb[model][:], in_=rows_of(x, model))
         for g in range(PASSES):
             load_wo(PASSES + g)
         load_planes(wgu_planes, W_gu_scales)
@@ -104,7 +113,7 @@ def tile_twomodelblockrouted_pb_e_kernel(
                     )
 
         def quantise_rows(rows_bf16, codes, planes):
-            words = rows_bf16[:].bitcast(F32)
+            words = rows_bf16.bitcast(F32)
             turned = banks.tile([P, PASSES, 2, P], F32, tag="bank")
             for g in range(PASSES):
                 for u in range(2):
@@ -122,21 +131,22 @@ def tile_twomodelblockrouted_pb_e_kernel(
             )
 
         def mx_operand(name):
-            codes = [
-                keep.tile([P, PASSES, P], U32, name="%s_codes_%d" % (name, rt), align_bytes=64)
-                for rt in range(ROW_TILES)
-            ]
-            planes = [
-                keep.tile([P, PASSES, P], U8, name="%s_planes_%d" % (name, rt), align_bytes=64)
-                for rt in range(ROW_TILES)
-            ]
+            codes = {}
+            planes = {}
+            for e, t in ROW_TILES:
+                codes[(e, t)] = keep.tile(
+                    [P, PASSES, P], U32, name="%s_codes_%d_%d" % (name, e, t), align_bytes=64
+                )
+                planes[(e, t)] = keep.tile(
+                    [P, PASSES, P], U8, name="%s_planes_%d_%d" % (name, e, t), align_bytes=64
+                )
             return codes, planes
 
         a_codes, a_planes = mx_operand("a")
         h_codes, h_planes = mx_operand("h")
 
-        for rt in range(ROW_TILES):
-            quantise_rows(attn_sb[rt], a_codes[rt], a_planes[rt])
+        for e, t in ROW_TILES:
+            quantise_rows(attn_sb[e][:, t, :], a_codes[(e, t)], a_planes[(e, t)])
 
         gains = keep.tile([P, MODELS, H], BF16)
         for model in range(MODELS):
@@ -151,62 +161,62 @@ def tile_twomodelblockrouted_pb_e_kernel(
                 )
                 nc.scalar.copy(out=gains[:, model, N_BLOCK * nb : N_BLOCK * (nb + 1)], in_=spread[:])
 
-        xmid = [keep.tile([P, H], F32, name="xmid_%d" % rt) for rt in range(ROW_TILES)]
-        sumsq = keep.tile([P, ROW_TILES], F32)
-        rms = keep.tile([P, ROW_TILES], F32)
-        rstd = keep.tile([P, ROW_TILES], F32)
-        for rt in range(ROW_TILES):
+        xmid = per_model("xmid", H, F32)
+        sumsq = keep.tile([P, len(ROW_TILES)], F32)
+        rms = keep.tile([P, len(ROW_TILES)], F32)
+        rstd = keep.tile([P, len(ROW_TILES)], F32)
+        for i, (e, t) in enumerate(ROW_TILES):
             for nb in range(H // N_BLOCK):
                 cols = slice(N_BLOCK * nb, N_BLOCK * (nb + 1))
                 o_acc = banks.tile([P, N_BLOCK], F32, tag="bank")
                 for g in range(PASSES):
-                    group = PASSES * MODEL_OF_ROW_TILE[rt] + g
+                    group = PASSES * e + g
                     nc.tensor.matmul_mx(
                         out=o_acc[:],
-                        lhsT=a_codes[rt][:, g, :].bitcast(FP8X4),
-                        lhsT_scale=a_planes[rt][:, g, :],
+                        lhsT=a_codes[(e, t)][:, g, :].bitcast(FP8X4),
+                        lhsT_scale=a_planes[(e, t)][:, g, :],
                         rhs=wo_words[group][:, cols].bitcast(FP8X4),
                         rhs_scale=wo_planes[4 * group : P, cols],
                         start=(g == 0),
                         stop=(g == PASSES - 1),
                     )
                 nc.vector.tensor_tensor(
-                    out=xmid[rt][:, cols], in0=o_acc[:], in1=x_sb[rt][:, cols], op=ALU.add
+                    out=xmid[e][:, t, cols], in0=o_acc[:], in1=x_sb[e][:, t, cols], op=ALU.add
                 )
             squares = work.tile([P, H], BF16)
             nc.scalar.activation(
-                out=squares[:], in_=xmid[rt][:], func=ACT.Square, accum_out=sumsq[:, rt : rt + 1]
+                out=squares[:], in_=xmid[e][:, t, :], func=ACT.Square, accum_out=sumsq[:, i : i + 1]
             )
             nc.scalar.activation(
-                out=rms[:, rt : rt + 1],
-                in_=sumsq[:, rt : rt + 1],
+                out=rms[:, i : i + 1],
+                in_=sumsq[:, i : i + 1],
                 func=ACT.Sqrt,
                 scale=1.0 / H,
                 bias=eps[:],
             )
 
-        h_sb = [keep.tile([P, H], BF16, name="h_%d" % rt) for rt in range(ROW_TILES)]
-        for rt in range(ROW_TILES):
-            nc.vector.reciprocal(out=rstd[:, rt : rt + 1], in_=rms[:, rt : rt + 1])
+        h_sb = per_model("h", H, BF16)
+        for i, (e, t) in enumerate(ROW_TILES):
+            nc.vector.reciprocal(out=rstd[:, i : i + 1], in_=rms[:, i : i + 1])
             nc.vector.scalar_tensor_tensor(
-                out=h_sb[rt][:],
-                in0=xmid[rt][:],
-                scalar=rstd[:, rt : rt + 1],
-                in1=gains[:, MODEL_OF_ROW_TILE[rt], :],
+                out=h_sb[e][:, t, :],
+                in0=xmid[e][:, t, :],
+                scalar=rstd[:, i : i + 1],
+                in1=gains[:, e, :],
                 op0=ALU.mult,
                 op1=ALU.mult,
             )
-        for rt in range(ROW_TILES):
-            quantise_rows(h_sb[rt], h_codes[rt], h_planes[rt])
+        for e, t in ROW_TILES:
+            quantise_rows(h_sb[e][:, t, :], h_codes[(e, t)], h_planes[(e, t)])
 
-        def project(rt, first, blk, side):
+        def project(e, t, first, blk, side):
             acc = banks.tile([P, N_BLOCK], F32, tag="bank")
             for g in range(PASSES):
-                group = PASSES * MODEL_OF_ROW_TILE[rt] + g
+                group = PASSES * e + g
                 nc.tensor.matmul_mx(
                     out=acc[:],
-                    lhsT=h_codes[rt][:, g, :].bitcast(FP8X4),
-                    lhsT_scale=h_planes[rt][:, g, :],
+                    lhsT=h_codes[(e, t)][:, g, :].bitcast(FP8X4),
+                    lhsT_scale=h_planes[(e, t)][:, g, :],
                     rhs=wgu_words[(group, first)][
                         :, side, N_BLOCK * (blk - first) : N_BLOCK * (blk - first + 1)
                     ].bitcast(FP8X4),
@@ -218,23 +228,23 @@ def tile_twomodelblockrouted_pb_e_kernel(
                 )
             return acc
 
-        hmlp = [keep.tile([P, FF], F32, name="hmlp_%d" % rt) for rt in range(ROW_TILES)]
+        hmlp = per_model("hmlp", FF, F32)
         for model in range(MODELS):
             for first, last in GU_CHUNKS[model]:
-                for rt in ROW_TILES_OF_MODEL[model]:
+                for t in range(TILES_OF_MODEL[model]):
                     for blk in range(first, last):
-                        gate = project(rt, first, blk, 0)
-                        up = project(rt, first, blk, 1)
+                        gate = project(model, t, first, blk, 0)
+                        up = project(model, t, first, blk, 1)
                         silu_gate = work.tile([P, N_BLOCK], F32)
                         nc.scalar.activation(out=silu_gate[:], in_=gate[:], func=ACT.Silu)
                         nc.vector.tensor_tensor(
-                            out=hmlp[rt][:, N_BLOCK * blk : N_BLOCK * (blk + 1)],
+                            out=hmlp[model][:, t, N_BLOCK * blk : N_BLOCK * (blk + 1)],
                             in0=silu_gate[:],
                             in1=up[:],
                             op=ALU.mult,
                         )
 
-        for rt in range(ROW_TILES):
-            nc.sync.dma_start(out=out_0[P * rt : P * (rt + 1), :], in_=xmid[rt][:])
-        for rt in range(ROW_TILES):
-            nc.sync.dma_start(out=out_1[P * rt : P * (rt + 1), :], in_=hmlp[rt][:])
+        for model in range(MODELS):
+            nc.sync.dma_start(out=rows_of(out_0, model), in_=xmid[model][:])
+        for model in range(MODELS):
+            nc.sync.dma_start(out=rows_of(out_1, model), in_=hmlp[model][:])

@@ -246,5 +246,8 @@ def tile_twomodelblockrouted_pb_e_kernel(
 
         for model in range(MODELS):
             nc.sync.dma_start(out=rows_of(out_0, model), in_=xmid[model][:])
-        for model in range(MODELS):
-            nc.sync.dma_start(out=rows_of(out_1, model), in_=hmlp[model][:])
+        for e, t in ROW_TILES:
+            pieces = ((0, FF_BLOCKS),) if e == 0 else ((0, 3), (3, FF_BLOCKS))
+            for first, last in pieces:
+                cols = slice(N_BLOCK * first, N_BLOCK * last)
+                nc.sync.dma_start(out=rows_of(out_1, e)[:, t, cols], in_=hmlp[e][:, t, cols])

@@ -88,13 +88,13 @@ def tile_twomodelblockrouted_pb_e_kernel(
         for model in range(MODELS):
             nc.sync.dma_start(out=attn_sb[model][:], in_=rows_of(attn, model))
         load_planes(wo_planes, W_o_scales)
+        load_planes(wgu_planes, W_gu_scales)
         for g in range(PASSES):
             load_wo(g)
         for model in range(MODELS):
             nc.sync.dma_start(out=x_sb[model][:], in_=rows_of(x, model))
         for g in range(PASSES):
             load_wo(PASSES + g)
-        load_planes(wgu_planes, W_gu_scales)
         for model in range(MODELS):
             for first, last in GU_CHUNKS[model]:
                 for g in range(PASSES):

@@ -46,10 +46,10 @@ def tile_twomodelblockrouted_pb_e_kernel(
         eps = keep.tile([P, 1], F32)
         ident = keep.tile([P, P], F32)
         nc.vector.memset(wo_planes[:].bitcast(I32), 0)
-        nc.vector.memset(ln2_row[:], 0.0)
+        nc.vector.memset(wgu_planes[:].bitcast(I32), 0)
+        nc.vector.memset(ln2_row[:].bitcast(I32), 0)
         nc.vector.memset(ones[:], 1.0)
         nc.vector.memset(eps[:], EPS)
-        nc.vector.memset(wgu_planes[:].bitcast(I32), 0)
         make_identity(nc, ident[:])
 
         def load_planes(planes, scales):

@@ -41,16 +41,18 @@ def tile_twomodelblockrouted_pb_e_kernel(
 
         wo_planes = keep.tile([P, H], U8, align_bytes=64)
         wgu_planes = keep.tile([P, 2 * FF], U8, align_bytes=64)
-        ln2_row = keep.tile([P, MODELS * H], BF16)
-        ones = keep.tile([P, P], BF16)
-        eps = keep.tile([P, 1], F32)
+        ln2_rows = keep.tile([P, P], BF16)
+        one = keep.tile([P, 1], F32)
+        minus_half = keep.tile([P, 1], F32)
         ident = keep.tile([P, P], F32)
+        ident_bf16 = keep.tile([P, P], BF16)
+        nc.vector.memset(ln2_rows[:], 0.0)
+        nc.vector.memset(one[:], 1.0)
         nc.vector.memset(wo_planes[:].bitcast(I32), 0)
         nc.vector.memset(wgu_planes[:].bitcast(I32), 0)
-        nc.vector.memset(ln2_row[:].bitcast(I32), 0)
-        nc.vector.memset(ones[:], 1.0)
-        nc.vector.memset(eps[:], EPS)
+        nc.vector.memset(minus_half[:], -0.5)
         make_identity(nc, ident[:])
+        nc.vector.tensor_copy(out=ident_bf16[:], in_=ident[:])
 
         def load_planes(planes, scales):
             for quadrant in range(4):
@@ -58,12 +60,6 @@ def tile_twomodelblockrouted_pb_e_kernel(
                     out=planes[32 * quadrant : 32 * quadrant + 16, :].bitcast(I32),
                     in_=scales[:, 4 * quadrant : 4 * quadrant + 4, :].bitcast(I32),
                 )
-
-        def load_wo(group):
-            nc.sync.dma_start(
-                out=wo_words[group][:].bitcast(I32),
-                in_=W_o_words[group].rearrange("p n t -> p (n t)").bitcast(I32),
-            )
 
         def rows_of(dram, model):
             return dram[FIRST_ROW[model] : FIRST_ROW[model + 1], :].rearrange(
@@ -79,40 +75,61 @@ def tile_twomodelblockrouted_pb_e_kernel(
         attn_sb = per_model("attn", H, BF16)
         x_sb = per_model("x", H, BF16)
         wo_words = [
-            keep.tile([P, H], U32, name="wo_%d" % group, align_bytes=64)
-            for group in range(MODELS * PASSES)
+            keep.tile([P, PASSES, H], U32, name="wo_%d" % e, align_bytes=64) for e in range(MODELS)
         ]
         wgu_words = {}
 
-        nc.scalar.dma_start(out=ln2_row[0:1, :], in_=ln2.rearrange("e k -> (e k)").unsqueeze(0))
-        for model in range(MODELS):
+        def load_attn(model):
             nc.sync.dma_start(out=attn_sb[model][:], in_=rows_of(attn, model))
+
+        def load_wo(model):
+            nc.sync.dma_start(
+                out=wo_words[model][:].bitcast(I32),
+                in_=W_o_words[PASSES * model : PASSES * (model + 1)]
+                .rearrange("g p n t -> p g (n t)")
+                .bitcast(I32),
+            )
+
+        def load_x(model, first, last):
+            nc.sync.dma_start(
+                out=x_sb[model][:, first:last, :], in_=rows_of(x, model)[:, first:last, :]
+            )
+
+        def load_gu(model, first, last):
+            for group in range(PASSES * model, PASSES * (model + 1)):
+                chunk = keep.tile(
+                    [P, 2, (last - first) * N_BLOCK],
+                    U32,
+                    name="wgu_%d_%d" % (group, first),
+                    align_bytes=64,
+                )
+                wgu_words[(group, first)] = chunk
+                halves = W_gu_words[group].rearrange("p (s n) t -> p s (n t)", s=2)
+                nc.sync.dma_start(
+                    out=chunk[:].bitcast(I32),
+                    in_=halves[:, :, PACK * N_BLOCK * first : PACK * N_BLOCK * last].bitcast(I32),
+                )
+
+        nc.scalar.dma_start(
+            out=ln2_rows[0 : MODELS * H // P, :], in_=ln2.rearrange("e (c k) -> (e c) k", k=P)
+        )
+        table = keep.tile([P, 1], F32)
+        nc.scalar.activation(out=table[:], in_=one[:], func=ACT.Sqrt)
+        load_attn(0)
         load_planes(wo_planes, W_o_scales)
         load_planes(wgu_planes, W_gu_scales)
-        for g in range(PASSES):
-            load_wo(g)
-        for model in range(MODELS):
-            nc.sync.dma_start(out=x_sb[model][:], in_=rows_of(x, model))
-        for g in range(PASSES):
-            load_wo(PASSES + g)
-        for model in range(MODELS):
-            for first, last in GU_CHUNKS[model]:
-                for g in range(PASSES):
-                    group = PASSES * model + g
-                    chunk = keep.tile(
-                        [P, 2, (last - first) * N_BLOCK],
-                        U32,
-                        name="wgu_%d_%d" % (group, first),
-                        align_bytes=64,
-                    )
-                    wgu_words[(group, first)] = chunk
-                    halves = W_gu_words[group].rearrange("p (s n) t -> p s (n t)", s=2)
-                    nc.sync.dma_start(
-                        out=chunk[:].bitcast(I32),
-                        in_=halves[:, :, PACK * N_BLOCK * first : PACK * N_BLOCK * last].bitcast(I32),
-                    )
+        load_wo(0)
+        load_x(0, 0, 1)
+        load_x(0, 1, TILES_OF_MODEL[0])
+        load_attn(1)
+        load_gu(0, *GU_CHUNKS[0][0])
+        load_wo(1)
+        load_x(1, 0, 1)
+        load_gu(0, *GU_CHUNKS[0][1])
+        for first, last in GU_CHUNKS[1]:
+            load_gu(1, first, last)
 
-        def quantise_rows(rows_bf16, codes, planes):
+        def turn_rows(rows_bf16):
             words = rows_bf16.bitcast(F32)
             turned = banks.tile([P, PASSES, 2, P], F32, tag="bank")
             for g in range(PASSES):
@@ -120,10 +137,16 @@ def tile_twomodelblockrouted_pb_e_kernel(
                     nc.tensor.transpose(
                         turned[:, g, u, :], words[:, 256 * g + u : 256 * (g + 1) : 2], ident[:]
                     )
+            return turned
+
+        def regroup(turned):
             grouped = work.tile([P, PASSES, P, PACK], BF16, align_bytes=64)
             nc.scalar.copy(
                 out=grouped[:].bitcast(F32), in_=turned[:].rearrange("p g u r -> p g r u")
             )
+            return grouped
+
+        def quantise(grouped, codes, planes):
             nc.vector.quantize_mx(
                 out=codes[:].rearrange("p g r -> p (g r)").bitcast(FP8X4),
                 scales=planes[:].rearrange("p g r -> p (g r)"),
@@ -144,28 +167,35 @@ def tile_twomodelblockrouted_pb_e_kernel(
 
         a_codes, a_planes = mx_operand("a")
         h_codes, h_planes = mx_operand("h")
-
-        for e, t in ROW_TILES:
-            quantise_rows(attn_sb[e][:, t, :], a_codes[(e, t)], a_planes[(e, t)])
-
         gains = keep.tile([P, MODELS, H], BF16)
-        for model in range(MODELS):
-            for nb in range(H // N_BLOCK):
-                spread = banks.tile([P, N_BLOCK], F32, tag="bank")
-                nc.tensor.matmul(
-                    out=spread[:],
-                    lhsT=ones[:],
-                    rhs=ln2_row[:, H * model + N_BLOCK * nb : H * model + N_BLOCK * (nb + 1)],
-                    start=True,
-                    stop=True,
-                )
-                nc.scalar.copy(out=gains[:, model, N_BLOCK * nb : N_BLOCK * (nb + 1)], in_=spread[:])
-
         xmid = per_model("xmid", H, F32)
-        sumsq = keep.tile([P, len(ROW_TILES)], F32)
+        h_sb = per_model("h", H, BF16)
+        hmlp = per_model("hmlp", FF, F32)
+        sumsq = keep.tile([P, len(ROW_TILES), H // N_BLOCK], F32)
+        half_mean = keep.tile([P, len(ROW_TILES)], F32)
         rms = keep.tile([P, len(ROW_TILES)], F32)
         rstd = keep.tile([P, len(ROW_TILES)], F32)
-        for i, (e, t) in enumerate(ROW_TILES):
+
+        def spread_gains():
+            for model in range(MODELS):
+                for nb in range(H // N_BLOCK):
+                    spread = banks.tile([P, N_BLOCK // P, P], F32, tag="bank")
+                    for c in range(N_BLOCK // P):
+                        r = (H * model + N_BLOCK * nb) // P + c
+                        nc.tensor.matmul(
+                            out=spread[:, c, :],
+                            lhsT=ident_bf16[:, r : r + 1].to_broadcast([P, P]),
+                            rhs=ln2_rows[:],
+                            start=True,
+                            stop=True,
+                        )
+                    nc.scalar.copy(
+                        out=gains[:, model, N_BLOCK * nb : N_BLOCK * (nb + 1)],
+                        in_=spread[:].rearrange("p c k -> p (c k)"),
+                    )
+
+        def project_attn(e, t):
+            halves = []
             for nb in range(H // N_BLOCK):
                 cols = slice(N_BLOCK * nb, N_BLOCK * (nb + 1))
                 o_acc = banks.tile([P, N_BLOCK], F32, tag="bank")
@@ -175,39 +205,77 @@ def tile_twomodelblockrouted_pb_e_kernel(
                         out=o_acc[:],
                         lhsT=a_codes[(e, t)][:, g, :].bitcast(FP8X4),
                         lhsT_scale=a_planes[(e, t)][:, g, :],
-                        rhs=wo_words[group][:, cols].bitcast(FP8X4),
+                        rhs=wo_words[e][:, g, cols].bitcast(FP8X4),
                         rhs_scale=wo_planes[4 * group : P, cols],
                         start=(g == 0),
                         stop=(g == PASSES - 1),
                     )
-                nc.vector.tensor_tensor(
-                    out=xmid[e][:, t, cols], in0=o_acc[:], in1=x_sb[e][:, t, cols], op=ALU.add
-                )
-            squares = work.tile([P, H], BF16)
-            nc.scalar.activation(
-                out=squares[:], in_=xmid[e][:, t, :], func=ACT.Square, accum_out=sumsq[:, i : i + 1]
+                halves.append(o_acc)
+            return halves
+
+        def add_x(e, t, nb, o_acc):
+            i = ROW_TILES.index((e, t))
+            cols = slice(N_BLOCK * nb, N_BLOCK * (nb + 1))
+            nc.vector.tensor_tensor(
+                out=xmid[e][:, t, cols], in0=o_acc[:], in1=x_sb[e][:, t, cols], op=ALU.add
             )
+            squares = work.tile([P, N_BLOCK], BF16)
+            nc.scalar.activation(
+                out=squares[:],
+                in_=xmid[e][:, t, cols],
+                func=ACT.Square,
+                accum_out=sumsq[:, i, nb : nb + 1],
+            )
+            if nb == 0:
+                nc.scalar.activation(
+                    out=half_mean[:, i : i + 1],
+                    in_=sumsq[:, i, 0:1],
+                    func=ACT.Copy,
+                    scale=1.0 / H,
+                    bias=EPS,
+                )
+
+        def root_by_scalar(e, t):
+            i = ROW_TILES.index((e, t))
             nc.scalar.activation(
                 out=rms[:, i : i + 1],
-                in_=sumsq[:, i : i + 1],
+                in_=sumsq[:, i, 1:2],
                 func=ACT.Sqrt,
                 scale=1.0 / H,
-                bias=eps[:],
+                bias=half_mean[:, i : i + 1],
             )
 
-        h_sb = per_model("h", H, BF16)
-        for i, (e, t) in enumerate(ROW_TILES):
+        def invert(e, t):
+            i = ROW_TILES.index((e, t))
             nc.vector.reciprocal(out=rstd[:, i : i + 1], in_=rms[:, i : i + 1])
-            nc.vector.scalar_tensor_tensor(
-                out=h_sb[e][:, t, :],
-                in0=xmid[e][:, t, :],
-                scalar=rstd[:, i : i + 1],
-                in1=gains[:, e, :],
+
+        def root_by_gpsimd(e, t):
+            i = ROW_TILES.index((e, t))
+            column = slice(i, i + 1)
+            nc.gpsimd.tensor_scalar(
+                out=rms[:, column],
+                in0=sumsq[:, i, 1:2],
+                scalar1=1.0 / H,
+                scalar2=half_mean[:, column],
                 op0=ALU.mult,
-                op1=ALU.mult,
+                op1=ALU.add,
             )
-        for e, t in ROW_TILES:
-            quantise_rows(h_sb[e][:, t, :], h_codes[(e, t)], h_planes[(e, t)])
+            nc.gpsimd.tensor_tensor(
+                out=rstd[:, column], in0=rms[:, column], in1=minus_half[:], op=ALU.pow
+            )
+
+        def norm(e, t):
+            i = ROW_TILES.index((e, t))
+            for nb in range(H // N_BLOCK):
+                cols = slice(N_BLOCK * nb, N_BLOCK * (nb + 1))
+                nc.vector.scalar_tensor_tensor(
+                    out=h_sb[e][:, t, cols],
+                    in0=xmid[e][:, t, cols],
+                    scalar=rstd[:, i : i + 1],
+                    in1=gains[:, e, cols],
+                    op0=ALU.mult,
+                    op1=ALU.mult,
+                )
 
         def project(e, t, first, blk, side):
             acc = banks.tile([P, N_BLOCK], F32, tag="bank")
@@ -228,21 +296,74 @@ def tile_twomodelblockrouted_pb_e_kernel(
                 )
             return acc
 
-        hmlp = per_model("hmlp", FF, F32)
-        for model in range(MODELS):
-            for first, last in GU_CHUNKS[model]:
-                for t in range(TILES_OF_MODEL[model]):
-                    for blk in range(first, last):
-                        gate = project(model, t, first, blk, 0)
-                        up = project(model, t, first, blk, 1)
-                        silu_gate = work.tile([P, N_BLOCK], F32)
-                        nc.scalar.activation(out=silu_gate[:], in_=gate[:], func=ACT.Silu)
-                        nc.vector.tensor_tensor(
-                            out=hmlp[model][:, t, N_BLOCK * blk : N_BLOCK * (blk + 1)],
-                            in0=silu_gate[:],
-                            in1=up[:],
-                            op=ALU.mult,
-                        )
+        def gated(e, t, first, last):
+            for blk in range(first, last):
+                gate = project(e, t, first, blk, 0)
+                up = project(e, t, first, blk, 1)
+                silu_gate = work.tile([P, N_BLOCK], F32)
+                nc.scalar.activation(out=silu_gate[:], in_=gate[:], func=ACT.Silu)
+                nc.vector.tensor_tensor(
+                    out=hmlp[e][:, t, N_BLOCK * blk : N_BLOCK * (blk + 1)],
+                    in0=silu_gate[:],
+                    in1=up[:],
+                    op=ALU.mult,
+                )
+
+        def turn_attn(e, t):
+            return turn_rows(attn_sb[e][:, t, :])
+
+        def turn_h(e, t):
+            return turn_rows(h_sb[e][:, t, :])
+
+        def quantise_attn(e, t, grouped):
+            quantise(grouped, a_codes[(e, t)], a_planes[(e, t)])
+
+        def quantise_h(e, t, grouped):
+            quantise(grouped, h_codes[(e, t)], h_planes[(e, t)])
+
+        attn_turned = [turn_attn(0, t) for t in range(TILES_OF_MODEL[0])]
+        for t in range(TILES_OF_MODEL[0]):
+            quantise_attn(0, t, regroup(attn_turned[t]))
+        spread_gains()
+        o_halves = [project_attn(0, t) for t in range(TILES_OF_MODEL[0])]
+        attn_turned_1 = turn_attn(1, 0)
+        for t in range(2):
+            for nb in range(2):
+                add_x(0, t, nb, o_halves[t][nb])
+            root_by_scalar(0, t)
+        invert(0, 0)
+        norm(0, 0)
+        grouped_00 = regroup(turn_h(0, 0))
+        invert(0, 1)
+        norm(0, 1)
+        add_x(0, 2, 0, o_halves[2][0])
+        grouped_01 = regroup(turn_h(0, 1))
+        quantise_h(0, 0, grouped_00)
+        add_x(0, 2, 1, o_halves[2][1])
+        root_by_scalar(0, 2)
+        attn_grouped_1 = regroup(attn_turned_1)
+        quantise_h(0, 1, grouped_01)
+        invert(0, 2)
+        norm(0, 2)
+
+        chunk_a, chunk_b = GU_CHUNKS[0]
+        gated(0, 0, *chunk_a)
+        grouped_02 = regroup(turn_h(0, 2))
+        quantise_h(0, 2, grouped_02)
+        quantise_attn(1, 0, attn_grouped_1)
+        gated(0, 1, *chunk_a)
+        o_halves_1 = project_attn(1, 0)
+        for nb in range(2):
+            add_x(1, 0, nb, o_halves_1[nb])
+        gated(0, 2, *chunk_a)
+        root_by_gpsimd(1, 0)
+        gated(0, 0, *chunk_b)
+        norm(1, 0)
+        gated(0, 1, *chunk_b)
+        grouped_10 = regroup(turn_h(1, 0))
+        quantise_h(1, 0, grouped_10)
+        gated(0, 2, *chunk_b)
+        gated(1, 0, *GU_CHUNKS[1][0])
 
         for model in range(MODELS):
             nc.sync.dma_start(out=rows_of(out_0, model), in_=xmid[model][:])

@@ -48,17 +48,17 @@ def tile_twomodelblockrouted_pb_e_kernel(
         ident_bf16 = keep.tile([P, P], BF16)
         nc.vector.memset(ln2_rows[:], 0.0)
         nc.vector.memset(one[:], 1.0)
-        nc.vector.memset(wo_planes[:].bitcast(I32), 0)
         nc.vector.memset(wgu_planes[:].bitcast(I32), 0)
+        nc.vector.memset(wo_planes[:].bitcast(I32), 0)
         nc.vector.memset(minus_half[:], -0.5)
         make_identity(nc, ident[:])
         nc.vector.tensor_copy(out=ident_bf16[:], in_=ident[:])
 
-        def load_planes(planes, scales):
+        def load_planes(planes, scales, first, last):
             for quadrant in range(4):
                 nc.sync.dma_start(
-                    out=planes[32 * quadrant : 32 * quadrant + 16, :].bitcast(I32),
-                    in_=scales[:, 4 * quadrant : 4 * quadrant + 4, :].bitcast(I32),
+                    out=planes[32 * quadrant : 32 * quadrant + 16, first:last].bitcast(I32),
+                    in_=scales[:, 4 * quadrant : 4 * quadrant + 4, first:last].bitcast(I32),
                 )
 
         def rows_of(dram, model):
@@ -116,12 +116,13 @@ def tile_twomodelblockrouted_pb_e_kernel(
         table = keep.tile([P, 1], F32)
         nc.scalar.activation(out=table[:], in_=one[:], func=ACT.Sqrt)
         load_attn(0)
-        load_planes(wo_planes, W_o_scales)
-        load_planes(wgu_planes, W_gu_scales)
+        load_attn(1)
+        load_planes(wgu_planes, W_gu_scales, 0, FF)
+        load_planes(wgu_planes, W_gu_scales, FF, 2 * FF)
+        load_planes(wo_planes, W_o_scales, 0, H)
         load_wo(0)
         load_x(0, 0, 1)
         load_x(0, 1, TILES_OF_MODEL[0])
-        load_attn(1)
         load_gu(0, *GU_CHUNKS[0][0])
         load_wo(1)
         load_x(1, 0, 1)

from contextlib import ExitStack

import concourse.mybir as mybir
from concourse.masks import make_identity

F32 = mybir.dt.float32
BF16 = mybir.dt.bfloat16
I32 = mybir.dt.int32
U32 = mybir.dt.uint32
U8 = mybir.dt.uint8
FP8X4 = mybir.dt.float8_e4m3fn_x4
ACT = mybir.ActivationFunctionType
ALU = mybir.AluOpType

P = 128
ROWS, SPLIT, H, FF = 512, 384, 1024, 2560
MODELS = 2
EPS = 1.1920929e-07
PACK = 4
K_PASS = P * PACK
PASSES = H // K_PASS
N_BLOCK = 512
FIRST_ROW = (0, SPLIT, ROWS)
TILES_OF_MODEL = tuple((FIRST_ROW[e + 1] - FIRST_ROW[e]) // P for e in range(MODELS))
ROW_TILES = tuple((e, t) for e in range(MODELS) for t in range(TILES_OF_MODEL[e]))
FF_BLOCKS = FF // N_BLOCK
GU_CHUNKS = (((0, 2), (2, FF_BLOCKS)), ((0, FF_BLOCKS),))

FLOPS = 2 * ROWS * H * H + 2 * ROWS * H * 2 * FF


def tile_twomodelblockrouted_pb_e_kernel(
    tc, attn, x, W_o_words, W_o_scales, W_gu_words, W_gu_scales, ln2, out_0, out_1
):
    nc = tc.nc
    with ExitStack() as stack:
        stack.enter_context(tc.manual_schedule())
        keep = stack.enter_context(tc.tile_pool(name="keep", bufs=1))
        work = stack.enter_context(tc.tile_pool(name="work", bufs=3))
        banks = stack.enter_context(tc.psum_pool(name="banks", bufs=8))

        wo_planes = keep.tile([P, H], U8, align_bytes=64)
        wgu_planes = keep.tile([P, 2 * FF], U8, align_bytes=64)
        ln2_rows = keep.tile([P, P], BF16)
        one = keep.tile([P, 1], F32)
        minus_half = keep.tile([P, 1], F32)
        ident = keep.tile([P, P], F32)
        ident_bf16 = keep.tile([P, P], BF16)
        nc.vector.memset(ln2_rows[:], 0.0)
        nc.vector.memset(one[:], 1.0)
        nc.vector.memset(wgu_planes[:].bitcast(I32), 0)
        nc.vector.memset(wo_planes[:].bitcast(I32), 0)
        nc.vector.memset(minus_half[:], -0.5)
        make_identity(nc, ident[:])
        nc.vector.tensor_copy(out=ident_bf16[:], in_=ident[:])

        def load_planes(planes, scales, first, last):
            for quadrant in range(4):
                nc.sync.dma_start(
                    out=planes[32 * quadrant : 32 * quadrant + 16, first:last].bitcast(I32),
                    in_=scales[:, 4 * quadrant : 4 * quadrant + 4, first:last].bitcast(I32),
                )

        def rows_of(dram, model):
            return dram[FIRST_ROW[model] : FIRST_ROW[model + 1], :].rearrange(
                "(p t) c -> p t c", t=TILES_OF_MODEL[model]
            )

        def per_model(name, width, dtype):
            return [
                keep.tile([P, TILES_OF_MODEL[e], width], dtype, name="%s_%d" % (name, e))
                for e in range(MODELS)
            ]

        attn_sb = per_model("attn", H, BF16)
        x_sb = per_model("x", H, BF16)
        wo_words = [
            keep.tile([P, PASSES, H], U32, name="wo_%d" % e, align_bytes=64) for e in range(MODELS)
        ]
        wgu_words = {}

        def load_attn(model):
            nc.sync.dma_start(out=attn_sb[model][:], in_=rows_of(attn, model))

        def load_wo(model):
            nc.sync.dma_start(
                out=wo_words[model][:].bitcast(I32),
                in_=W_o_words[PASSES * model : PASSES * (model + 1)]
                .rearrange("g p n t -> p g (n t)")
                .bitcast(I32),
            )

        def load_x(model, first, last):
            nc.sync.dma_start(
                out=x_sb[model][:, first:last, :], in_=rows_of(x, model)[:, first:last, :]
            )

        def load_gu(model, first, last):
            for group in range(PASSES * model, PASSES * (model + 1)):
                chunk = keep.tile(
                    [P, 2, (last - first) * N_BLOCK],
                    U32,
                    name="wgu_%d_%d" % (group, first),
                    align_bytes=64,
                )
                wgu_words[(group, first)] = chunk
                halves = W_gu_words[group].rearrange("p (s n) t -> p s (n t)", s=2)
                nc.sync.dma_start(
                    out=chunk[:].bitcast(I32),
                    in_=halves[:, :, PACK * N_BLOCK * first : PACK * N_BLOCK * last].bitcast(I32),
                )

        nc.scalar.dma_start(
            out=ln2_rows[0 : MODELS * H // P, :], in_=ln2.rearrange("e (c k) -> (e c) k", k=P)
        )
        table = keep.tile([P, 1], F32)
        nc.scalar.activation(out=table[:], in_=one[:], func=ACT.Sqrt)
        load_attn(0)
        load_attn(1)
        load_planes(wgu_planes, W_gu_scales, 0, FF)
        load_planes(wgu_planes, W_gu_scales, FF, 2 * FF)
        load_planes(wo_planes, W_o_scales, 0, H)
        load_wo(0)
        load_x(0, 0, 1)
        load_x(0, 1, TILES_OF_MODEL[0])
        load_gu(0, *GU_CHUNKS[0][0])
        load_wo(1)
        load_x(1, 0, 1)
        load_gu(0, *GU_CHUNKS[0][1])
        for first, last in GU_CHUNKS[1]:
            load_gu(1, first, last)

        def turn_rows(rows_bf16):
            words = rows_bf16.bitcast(F32)
            turned = banks.tile([P, PASSES, 2, P], F32, tag="bank")
            for g in range(PASSES):
                for u in range(2):
                    nc.tensor.transpose(
                        turned[:, g, u, :], words[:, 256 * g + u : 256 * (g + 1) : 2], ident[:]
                    )
            return turned

        def regroup(turned):
            grouped = work.tile([P, PASSES, P, PACK], BF16, align_bytes=64)
            nc.scalar.copy(
                out=grouped[:].bitcast(F32), in_=turned[:].rearrange("p g u r -> p g r u")
            )
            return grouped

        def quantise(grouped, codes, planes):
            nc.vector.quantize_mx(
                out=codes[:].rearrange("p g r -> p (g r)").bitcast(FP8X4),
                scales=planes[:].rearrange("p g r -> p (g r)"),
                in_=grouped[:].rearrange("p g r t -> p (g r t)"),
            )

        def mx_operand(name):
            codes = {}
            planes = {}
            for e, t in ROW_TILES:
                codes[(e, t)] = keep.tile(
                    [P, PASSES, P], U32, name="%s_codes_%d_%d" % (name, e, t), align_bytes=64
                )
                planes[(e, t)] = keep.tile(
                    [P, PASSES, P], U8, name="%s_planes_%d_%d" % (name, e, t), align_bytes=64
                )
            return codes, planes

        a_codes, a_planes = mx_operand("a")
        h_codes, h_planes = mx_operand("h")
        gains = keep.tile([P, MODELS, H], BF16)
        xmid = per_model("xmid", H, F32)
        h_sb = per_model("h", H, BF16)
        hmlp = per_model("hmlp", FF, F32)
        sumsq = keep.tile([P, len(ROW_TILES), H // N_BLOCK], F32)
        half_mean = keep.tile([P, len(ROW_TILES)], F32)
        rms = keep.tile([P, len(ROW_TILES)], F32)
        rstd = keep.tile([P, len(ROW_TILES)], F32)

        def spread_gains():
            for model in range(MODELS):
                for nb in range(H // N_BLOCK):
                    spread = banks.tile([P, N_BLOCK // P, P], F32, tag="bank")
                    for c in range(N_BLOCK // P):
                        r = (H * model + N_BLOCK * nb) // P + c
                        nc.tensor.matmul(
                            out=spread[:, c, :],
                            lhsT=ident_bf16[:, r : r + 1].to_broadcast([P, P]),
                            rhs=ln2_rows[:],
                            start=True,
                            stop=True,
                        )
                    nc.scalar.copy(
                        out=gains[:, model, N_BLOCK * nb : N_BLOCK * (nb + 1)],
                        in_=spread[:].rearrange("p c k -> p (c k)"),
                    )

        def project_attn(e, t):
            halves = []
            for nb in range(H // N_BLOCK):
                cols = slice(N_BLOCK * nb, N_BLOCK * (nb + 1))
                o_acc = banks.tile([P, N_BLOCK], F32, tag="bank")
                for g in range(PASSES):
                    group = PASSES * e + g
                    nc.tensor.matmul_mx(
                        out=o_acc[:],
                        lhsT=a_codes[(e, t)][:, g, :].bitcast(FP8X4),
                        lhsT_scale=a_planes[(e, t)][:, g, :],
                        rhs=wo_words[e][:, g, cols].bitcast(FP8X4),
                        rhs_scale=wo_planes[4 * group : P, cols],
                        start=(g == 0),
                        stop=(g == PASSES - 1),
                    )
                halves.append(o_acc)
            return halves

        def add_x(e, t, nb, o_acc):
            i = ROW_TILES.index((e, t))
            cols = slice(N_BLOCK * nb, N_BLOCK * (nb + 1))
            nc.vector.tensor_tensor(
                out=xmid[e][:, t, cols], in0=o_acc[:], in1=x_sb[e][:, t, cols], op=ALU.add
            )
            squares = work.tile([P, N_BLOCK], BF16)
            nc.scalar.activation(
                out=squares[:],
                in_=xmid[e][:, t, cols],
                func=ACT.Square,
                accum_out=sumsq[:, i, nb : nb + 1],
            )
            if nb == 0:
                nc.scalar.activation(
                    out=half_mean[:, i : i + 1],
                    in_=sumsq[:, i, 0:1],
                    func=ACT.Copy,
                    scale=1.0 / H,
                    bias=EPS,
                )

        def root_by_scalar(e, t):
            i = ROW_TILES.index((e, t))
            nc.scalar.activation(
                out=rms[:, i : i + 1],
                in_=sumsq[:, i, 1:2],
                func=ACT.Sqrt,
                scale=1.0 / H,
                bias=half_mean[:, i : i + 1],
            )

        def invert(e, t):
            i = ROW_TILES.index((e, t))
            nc.vector.reciprocal(out=rstd[:, i : i + 1], in_=rms[:, i : i + 1])

        def root_by_gpsimd(e, t):
            i = ROW_TILES.index((e, t))
            column = slice(i, i + 1)
            nc.gpsimd.tensor_scalar(
                out=rms[:, column],
                in0=sumsq[:, i, 1:2],
                scalar1=1.0 / H,
                scalar2=half_mean[:, column],
                op0=ALU.mult,
                op1=ALU.add,
            )
            nc.gpsimd.tensor_tensor(
                out=rstd[:, column], in0=rms[:, column], in1=minus_half[:], op=ALU.pow
            )

        def norm(e, t):
            i = ROW_TILES.index((e, t))
            for nb in range(H // N_BLOCK):
                cols = slice(N_BLOCK * nb, N_BLOCK * (nb + 1))
                nc.vector.scalar_tensor_tensor(
                    out=h_sb[e][:, t, cols],
                    in0=xmid[e][:, t, cols],
                    scalar=rstd[:, i : i + 1],
                    in1=gains[:, e, cols],
                    op0=ALU.mult,
                    op1=ALU.mult,
                )

        def project(e, t, first, blk, side):
            acc = banks.tile([P, N_BLOCK], F32, tag="bank")
            for g in range(PASSES):
                group = PASSES * e + g
                nc.tensor.matmul_mx(
                    out=acc[:],
                    lhsT=h_codes[(e, t)][:, g, :].bitcast(FP8X4),
                    lhsT_scale=h_planes[(e, t)][:, g, :],
                    rhs=wgu_words[(group, first)][
                        :, side, N_BLOCK * (blk - first) : N_BLOCK * (blk - first + 1)
                    ].bitcast(FP8X4),
                    rhs_scale=wgu_planes[
                        4 * group : P, FF * side + N_BLOCK * blk : FF * side + N_BLOCK * (blk + 1)
                    ],
                    start=(g == 0),
                    stop=(g == PASSES - 1),
                )
            return acc

        def gated(e, t, first, last):
            for blk in range(first, last):
                gate = project(e, t, first, blk, 0)
                up = project(e, t, first, blk, 1)
                silu_gate = work.tile([P, N_BLOCK], F32)
                nc.scalar.activation(out=silu_gate[:], in_=gate[:], func=ACT.Silu)
                nc.vector.tensor_tensor(
                    out=hmlp[e][:, t, N_BLOCK * blk : N_BLOCK * (blk + 1)],
                    in0=silu_gate[:],
                    in1=up[:],
                    op=ALU.mult,
                )

        def turn_attn(e, t):
            return turn_rows(attn_sb[e][:, t, :])

        def turn_h(e, t):
            return turn_rows(h_sb[e][:, t, :])

        def quantise_attn(e, t, grouped):
            quantise(grouped, a_codes[(e, t)], a_planes[(e, t)])

        def quantise_h(e, t, grouped):
            quantise(grouped, h_codes[(e, t)], h_planes[(e, t)])

        attn_turned = [turn_attn(0, t) for t in range(TILES_OF_MODEL[0])]
        for t in range(TILES_OF_MODEL[0]):
            quantise_attn(0, t, regroup(attn_turned[t]))
        spread_gains()
        o_halves = [project_attn(0, t) for t in range(TILES_OF_MODEL[0])]
        attn_turned_1 = turn_attn(1, 0)
        for t in range(2):
            for nb in range(2):
                add_x(0, t, nb, o_halves[t][nb])
            root_by_scalar(0, t)
        invert(0, 0)
        norm(0, 0)
        grouped_00 = regroup(turn_h(0, 0))
        invert(0, 1)
        norm(0, 1)
        add_x(0, 2, 0, o_halves[2][0])
        grouped_01 = regroup(turn_h(0, 1))
        quantise_h(0, 0, grouped_00)
        add_x(0, 2, 1, o_halves[2][1])
        root_by_scalar(0, 2)
        attn_grouped_1 = regroup(attn_turned_1)
        quantise_h(0, 1, grouped_01)
        invert(0, 2)
        norm(0, 2)

        chunk_a, chunk_b = GU_CHUNKS[0]
        gated(0, 0, *chunk_a)
        grouped_02 = regroup(turn_h(0, 2))
        quantise_h(0, 2, grouped_02)
        quantise_attn(1, 0, attn_grouped_1)
        gated(0, 1, *chunk_a)
        o_halves_1 = project_attn(1, 0)
        for nb in range(2):
            add_x(1, 0, nb, o_halves_1[nb])
        gated(0, 2, *chunk_a)
        root_by_gpsimd(1, 0)
        gated(0, 0, *chunk_b)
        norm(1, 0)
        gated(0, 1, *chunk_b)
        grouped_10 = regroup(turn_h(1, 0))
        quantise_h(1, 0, grouped_10)
        gated(0, 2, *chunk_b)
        gated(1, 0, *GU_CHUNKS[1][0])

        for model in range(MODELS):
            nc.sync.dma_start(out=rows_of(out_0, model), in_=xmid[model][:])
        for e, t in ROW_TILES:
            pieces = ((0, FF_BLOCKS),) if e == 0 else ((0, 3), (3, FF_BLOCKS))
            for first, last in pieces:
                cols = slice(N_BLOCK * first, N_BLOCK * last)
                nc.sync.dma_start(out=rows_of(out_1, e)[:, t, cols], in_=hmlp[e][:, t, cols])
